import numpy as np
import ml_dtypes


def mxq(x, axis, fmt="e4m3"):
    dtype, down = {"e4m3": (ml_dtypes.float8_e4m3fn, 7), "e5m2": (ml_dtypes.float8_e5m2, 14)}[fmt]
    v = np.moveaxis(np.asarray(x, np.float32).astype(ml_dtypes.bfloat16).astype(np.float64), axis, -1)
    blocks = v.reshape(v.shape[:-1] + (-1, 32))
    amax = np.abs(blocks).max(-1, keepdims=True)
    byte = np.maximum(np.where(amax > 0, np.frexp(amax)[1] - 1 + 127, 0) - down, 1)
    scale = np.exp2(byte - 127.0)
    codes = (blocks / scale).astype(np.float32).astype(dtype).astype(np.float64)
    return np.moveaxis((codes * scale).reshape(v.shape), -1, axis)


WIDE = False


def mx_kscale(k):
    if not WIDE:
        return np.ones(k)
    levels = np.array([10, -10, 5, -5, 0])
    a = np.random.permutation(np.resize(levels, k // 512 * 4)).reshape(k // 512, 4)
    idx = np.arange(k)
    return np.exp2(a[idx // 512, idx % 128 // 32])


BF16 = ml_dtypes.bfloat16


def bf(x):
    return np.asarray(x, np.float32).astype(BF16)


def f64(x):
    return np.asarray(x).astype(np.float64)


B, N, F, D, DIM = 2, 512, 512, 2048, 32
EPS = 1e-6
RAD = 3.0


def expmap0_full(us):
    r = np.sqrt((us * us).sum(-1, keepdims=True))
    rs = np.maximum(r, EPS)
    x0 = 0.5 * (np.exp(r) + np.exp(-r))
    xs = (0.5 * (np.exp(rs) - np.exp(-rs)) / rs) * us
    return np.concatenate([x0, xs], axis=-1)


def setup_inputs():
    s = mx_kscale(F)
    amp = 0.5 + 0.5 * np.random.random((B, N, 1))
    return {"x": bf(np.random.standard_normal((B, N, F)) * amp * s),
            "w_sp": bf(np.random.standard_normal((F, D)) * RAD / np.sqrt(D * F) / s[:, None])}


def reference(x, w_sp):
    us = mxq(f64(x), 2, "e4m3") @ mxq(f64(w_sp), 0, "e4m3")
    return expmap0_full(us)

@@ -1,0 +1,221 @@
+from contextlib import ExitStack
+
+import concourse.mybir as mybir
+from concourse.masks import make_identity
+
+F32 = mybir.dt.float32
+BF16 = mybir.dt.bfloat16
+U32 = mybir.dt.uint32
+U8 = mybir.dt.uint8
+FP8X4 = mybir.dt.float8_e4m3fn_x4
+ALU = mybir.AluOpType
+ACT = mybir.ActivationFunctionType
+
+P = 128
+PACK = 4
+K = P * PACK
+ROWS = 1024
+ROW_TILES = ROWS // P
+PAIRS = ROW_TILES // 2
+D = 2048
+BANK = 512
+CHUNKS = D // BANK
+EPS = 1e-6
+VECTOR_COLS = 320
+EXP_AFTER = 2
+
+FLOPS = 2 * ROWS * K * D
+
+
+def tile_hgcn_pb_kernel(tc, x, w_sp, out):
+    nc = tc.nc
+    x_rows = x.flatten_outer_dims().rearrange("(p i) k -> p i k", i=ROW_TILES)
+    out_flat = out.flatten_outer_dims().rearrange("(p i) c -> p (i c)", i=ROW_TILES)
+    w_rows = w_sp.rearrange("(p t) c -> p t c", t=PACK)
+
+    with ExitStack() as ctx:
+        keep = ctx.enter_context(tc.tile_pool(name="keep", bufs=1))
+        stage = ctx.enter_context(tc.tile_pool(name="stage", bufs=CHUNKS))
+        norm_banks = ctx.enter_context(tc.psum_pool(name="norm_banks", bufs=4))
+        scale_banks = ctx.enter_context(tc.psum_pool(name="scale_banks", bufs=4))
+        ctx.enter_context(tc.manual_schedule())
+
+        x_raw = keep.tile([P, ROW_TILES, K], BF16)
+        w_raw = []
+
+        def load_x(b):
+            nc.sync.dma_start(out=x_raw[:, 2 * b : 2 * b + 2, :], in_=x_rows[:, 2 * b : 2 * b + 2, :])
+
+        load_x(0)
+        for c in range(CHUNKS):
+            raw = stage.tile([P, PACK, BANK], BF16, name="w_raw%d" % c, tag="w_raw")
+            nc.sync.dma_start(out=raw[:], in_=w_rows[:, :, c * BANK : (c + 1) * BANK])
+            w_raw.append(raw)
+        for b in range(1, PAIRS):
+            load_x(b)
+
+        ident = keep.tile([P, P], F32)
+        make_identity(nc, ident[:])
+        powers = keep.tile([P, 2], F32)
+        nc.vector.memset(powers[:, 0:1], 0.5)
+        nc.vector.memset(powers[:, 1:2], -0.5)
+        warm = keep.tile([P, 2], F32)
+        nc.vector.memset(warm[:, 0:1], 0.0)
+        nc.scalar.activation(out=warm[:, 1:2], in_=warm[:, 0:1], func=ACT.Exp)
+
+        x_words = x_raw[:].bitcast(F32).rearrange("p i (q u) -> p i u q", u=2)
+        x_grouped = keep.tile([P, ROW_TILES, P, PACK], BF16, align_bytes=64)
+        x_grouped_words = x_grouped[:].bitcast(F32)
+        x_codes = keep.tile([P, ROWS], U32, align_bytes=64)
+        x_scales = keep.tile([P, ROWS], U8, align_bytes=64)
+
+        def transpose_x(b):
+            xt = norm_banks.tile([P, 2, 2, P], F32, name="xt%d" % b, tag="bank")
+            for i in range(2):
+                for u in range(2):
+                    nc.tensor.transpose(xt[:, i, u, :], x_words[:, 2 * b + i, u, :], ident[:])
+            nc.scalar.copy(
+                out=x_grouped_words[:, 2 * b : 2 * b + 2, :, :],
+                in_=xt[:].rearrange("q i u r -> q i r u"),
+            )
+
+        def quantise_x(b):
+            cols = slice(2 * b * P, (2 * b + 2) * P)
+            nc.vector.quantize_mx(
+                out=x_codes[:, cols].bitcast(FP8X4),
+                scales=x_scales[:, cols],
+                in_=x_grouped[:, 2 * b : 2 * b + 2, :, :].rearrange("p i r t -> p (i r t)"),
+            )
+
+        w_codes = keep.tile([P, D], U32, align_bytes=64)
+        w_scales = keep.tile([P, D], U8, align_bytes=64)
+        w_grouped = []
+
+        def regroup(c):
+            grouped = stage.tile(
+                [P, BANK, PACK], BF16, name="w_grouped%d" % c, tag="w_grouped", align_bytes=64
+            )
+            w_grouped.append(grouped)
+            nc.vector.tensor_copy(
+                out=grouped[:, :VECTOR_COLS, :].rearrange("p (c i) t -> p c t i", i=4),
+                in_=w_raw[c][:, :, :VECTOR_COLS].rearrange("p t (c i) -> p c t i", i=4),
+            )
+            nc.scalar.copy(
+                out=grouped[:, VECTOR_COLS:, :].rearrange("p (c i) t -> p c t i", i=4),
+                in_=w_raw[c][:, :, VECTOR_COLS:].rearrange("p t (c i) -> p c t i", i=4),
+            )
+
+        def quantise_w(c):
+            cols = slice(c * BANK, (c + 1) * BANK)
+            nc.vector.quantize_mx(
+                out=w_codes[:, cols].bitcast(FP8X4),
+                scales=w_scales[:, cols],
+                in_=w_grouped[c][:].rearrange("p c t -> p (c t)"),
+            )
+
+        result = keep.tile([P, ROW_TILES, 1 + D], F32)
+        result_flat = result[:].rearrange("p i c -> p (i c)")
+        sumsq = keep.tile([P, ROW_TILES, CHUNKS], F32)
+        radius = keep.tile([P, ROW_TILES, 5], F32)
+        expo = keep.tile([P, ROW_TILES, 2], F32)
+        factor = keep.tile([P, ROW_TILES], F32)
+
+        def multiply(i, c, banks):
+            bank = banks.tile([P, BANK], F32, name="us%d_%d" % (i, c), tag="bank")
+            nc.tensor.matmul_mx(
+                out=bank[:],
+                lhsT=x_codes[:, i * P : (i + 1) * P].bitcast(FP8X4),
+                lhsT_scale=x_scales[:, i * P : (i + 1) * P],
+                rhs=w_codes[:, c * BANK : (c + 1) * BANK].bitcast(FP8X4),
+                rhs_scale=w_scales[:, c * BANK : (c + 1) * BANK],
+                start=True,
+                stop=True,
+            )
+            return bank
+
+        def square(i, c):
+            bank = multiply(i, c, norm_banks)
+            squares = stage.tile([P, BANK], BF16, name="squares%d_%d" % (i, c), tag="squares")
+            nc.scalar.activation(
+                out=squares[:], in_=bank[:], func=ACT.Square, accum_out=sumsq[:, i, c : c + 1]
+            )
+
+        def find_radius(i):
+            nc.gpsimd.tensor_scalar(
+                out=radius[:, i, 0:1],
+                in0=sumsq[:, i, 0:1],
+                scalar1=sumsq[:, i, 1:2],
+                scalar2=sumsq[:, i, 2:3],
+                op0=ALU.add,
+                op1=ALU.add,
+            )
+            nc.gpsimd.tensor_scalar(
+                out=radius[:, i, 1:2],
+                in0=radius[:, i, 0:1],
+                scalar1=sumsq[:, i, 3:4],
+                scalar2=EPS * EPS,
+                op0=ALU.add,
+                op1=ALU.max,
+            )
+            nc.gpsimd.tensor_tensor(
+                out=radius[:, i, 2:4], in0=radius[:, i, 1:2].to_broadcast([P, 2]), in1=powers[:], op=ALU.pow
+            )
+            nc.gpsimd.tensor_scalar_mul(out=radius[:, i, 4:5], in0=radius[:, i, 3:4], scalar1=0.5)
+
+        def lift(i):
+            nc.scalar.activation(out=expo[:, i, 0:1], in_=radius[:, i, 2:3], func=ACT.Exp)
+            nc.scalar.activation(out=expo[:, i, 1:2], in_=radius[:, i, 2:3], func=ACT.Exp, scale=-1.0)
+            nc.vector.scalar_tensor_tensor(
+                out=factor[:, i : i + 1],
+                in0=expo[:, i, 0:1],
+                scalar=expo[:, i, 1:2],
+                in1=radius[:, i, 4:5],
+                op0=ALU.subtract,
+                op1=ALU.mult,
+            )
+            nc.vector.tensor_scalar(
+                out=result[:, i, 0:1],
+                in0=expo[:, i, 0:1],
+                scalar1=expo[:, i, 1:2],
+                scalar2=0.5,
+                op0=ALU.add,
+                op1=ALU.mult,
+            )
+
+        def store(start, end):
+            nc.sync.dma_start(out=out_flat[:, start:end], in_=result_flat[:, start:end])
+
+        transpose_x(0)
+        regroup(0)
+        quantise_x(0)
+        regroup(1)
+        for c in range(CHUNKS):
+            quantise_w(c)
+            if c + 2 < CHUNKS:
+                regroup(c + 2)
+            square(0, c)
+        find_radius(0)
+
+        for s in range(1, ROW_TILES + 1):
+            last = s == ROW_TILES
+            if s % 2 == 1 and s + 1 < ROW_TILES:
+                transpose_x((s + 1) // 2)
+                quantise_x((s + 1) // 2)
+            scaled = []
+            for c in range(CHUNKS):
+                if c == (0 if last else EXP_AFTER):
+                    lift(s - 1)
+                if not last:
+                    square(s, c)
+                scaled.append(multiply(s - 1, c, scale_banks))
+            if not last:
+                find_radius(s)
+            for c in range(CHUNKS):
+                dest = result[:, s - 1, 1 + c * BANK : 1 + (c + 1) * BANK]
+                if last and c % 2 == 1:
+                    nc.scalar.activation(
+                        out=dest, in_=scaled[c][:], func=ACT.Copy, scale=factor[:, s - 1 : s]
+                    )
+                else:
+                    nc.vector.tensor_scalar_mul(out=dest, in0=scaled[c][:], scalar1=factor[:, s - 1 : s])
+            store((s - 1) * D, ROW_TILES * (1 + D) if last else s * D)

@@ -22,7 +22,7 @@ BANK = 512
 CHUNKS = D // BANK
 EPS = 1e-6
 VECTOR_COLS = 320
-EXP_AFTER = 2
+EXP_AFTER = 3
 
 FLOPS = 2 * ROWS * K * D
 
@@ -162,9 +162,11 @@ def tile_hgcn_pb_kernel(tc, x, w_sp, out):
             )
             nc.gpsimd.tensor_scalar_mul(out=radius[:, i, 4:5], in0=radius[:, i, 3:4], scalar1=0.5)
 
-        def lift(i):
+        def take_exps(i):
             nc.scalar.activation(out=expo[:, i, 0:1], in_=radius[:, i, 2:3], func=ACT.Exp)
             nc.scalar.activation(out=expo[:, i, 1:2], in_=radius[:, i, 2:3], func=ACT.Exp, scale=-1.0)
+
+        def find_factor(i):
             nc.vector.scalar_tensor_tensor(
                 out=factor[:, i : i + 1],
                 in0=expo[:, i, 0:1],
@@ -196,26 +198,33 @@ def tile_hgcn_pb_kernel(tc, x, w_sp, out):
             square(0, c)
         find_radius(0)
 
-        for s in range(1, ROW_TILES + 1):
-            last = s == ROW_TILES
+        for s in range(1, ROW_TILES + 2):
+            i = s - 2
+            last = i == ROW_TILES - 1
             if s % 2 == 1 and s + 1 < ROW_TILES:
                 transpose_x((s + 1) // 2)
                 quantise_x((s + 1) // 2)
-            scaled = []
+            products = []
             for c in range(CHUNKS):
-                if c == (0 if last else EXP_AFTER):
-                    lift(s - 1)
-                if not last:
+                if s <= ROW_TILES and c == (EXP_AFTER if s < ROW_TILES else 0):
+                    take_exps(s - 1)
+                if s < ROW_TILES:
                     square(s, c)
-                scaled.append(multiply(s - 1, c, scale_banks))
-            if not last:
+                if i >= 0:
+                    products.append(multiply(i, c, scale_banks))
+            if s < ROW_TILES:
                 find_radius(s)
+            if i < 0:
+                continue
+            find_factor(i)
             for c in range(CHUNKS):
-                dest = result[:, s - 1, 1 + c * BANK : 1 + (c + 1) * BANK]
+                dest = result[:, i, 1 + c * BANK : 1 + (c + 1) * BANK]
                 if last and c % 2 == 1:
-                    nc.scalar.activation(
-                        out=dest, in_=scaled[c][:], func=ACT.Copy, scale=factor[:, s - 1 : s]
-                    )
+                    nc.scalar.activation(out=dest, in_=products[c][:], func=ACT.Copy, scale=factor[:, i : i + 1])
                 else:
-                    nc.vector.tensor_scalar_mul(out=dest, in0=scaled[c][:], scalar1=factor[:, s - 1 : s])
-            store((s - 1) * D, ROW_TILES * (1 + D) if last else s * D)
+                    nc.vector.tensor_scalar_mul(out=dest, in0=products[c][:], scalar1=factor[:, i : i + 1])
+                if last or c % 2 == 1:
+                    pieces = 1 if last else 2
+                    start = i * D + (c + 1 - pieces) * BANK
+                    end = ROW_TILES * (1 + D) if last and c + 1 == CHUNKS else i * D + (c + 1) * BANK
+                    store(start, end)

@@ -69,14 +69,19 @@ def tile_hgcn_pb_kernel(tc, x, w_sp, out):
         x_codes = keep.tile([P, ROWS], U32, align_bytes=64)
         x_scales = keep.tile([P, ROWS], U8, align_bytes=64)
 
-        def transpose_x(b):
-            xt = norm_banks.tile([P, 2, 2, P], F32, name="xt%d" % b, tag="bank")
+        x_transposed = {}
+
+        def transpose_x(b, banks):
+            xt = banks.tile([P, 2, 2, P], F32, name="xt%d" % b, tag="bank")
+            x_transposed[b] = xt
             for i in range(2):
                 for u in range(2):
                     nc.tensor.transpose(xt[:, i, u, :], x_words[:, 2 * b + i, u, :], ident[:])
-            nc.scalar.copy(
+
+        def group_x(b, copy):
+            copy(
                 out=x_grouped_words[:, 2 * b : 2 * b + 2, :, :],
-                in_=xt[:].rearrange("q i u r -> q i r u"),
+                in_=x_transposed[b][:].rearrange("q i u r -> q i r u"),
             )
 
         def quantise_x(b):
@@ -187,7 +192,8 @@ def tile_hgcn_pb_kernel(tc, x, w_sp, out):
         def store(start, end):
             nc.sync.dma_start(out=out_flat[:, start:end], in_=result_flat[:, start:end])
 
-        transpose_x(0)
+        transpose_x(0, norm_banks)
+        group_x(0, nc.scalar.copy)
         regroup(0)
         quantise_x(0)
         regroup(1)
@@ -196,14 +202,18 @@ def tile_hgcn_pb_kernel(tc, x, w_sp, out):
             if c + 2 < CHUNKS:
                 regroup(c + 2)
             square(0, c)
+            if c > 0:
+                transpose_x(c, scale_banks)
         find_radius(0)
+        group_x(1, nc.vector.tensor_copy)
+        for b in range(2, PAIRS):
+            group_x(b, nc.vector.tensor_copy)
+            quantise_x(b - 1)
+        quantise_x(PAIRS - 1)
 
         for s in range(1, ROW_TILES + 2):
             i = s - 2
             last = i == ROW_TILES - 1
-            if s % 2 == 1 and s + 1 < ROW_TILES:
-                transpose_x((s + 1) // 2)
-                quantise_x((s + 1) // 2)
             products = []
             for c in range(CHUNKS):
                 if s <= ROW_TILES and c == (EXP_AFTER if s < ROW_TILES else 0):

@@ -21,7 +21,7 @@ D = 2048
 BANK = 512
 CHUNKS = D // BANK
 EPS = 1e-6
-VECTOR_COLS = 320
+VECTOR_COLS = 352
 EXP_AFTER = 3
 
 FLOPS = 2 * ROWS * K * D
@@ -211,30 +211,36 @@ def tile_hgcn_pb_kernel(tc, x, w_sp, out):
             quantise_x(b - 1)
         quantise_x(PAIRS - 1)
 
+        def on_scalar(i, c):
+            return (i == ROW_TILES - 1 and c % 2 == 1) or (i == ROW_TILES - 2 and c >= CHUNKS - 2)
+
         for s in range(1, ROW_TILES + 2):
             i = s - 2
-            last = i == ROW_TILES - 1
+            squaring = s < ROW_TILES
             products = []
             for c in range(CHUNKS):
-                if s <= ROW_TILES and c == (EXP_AFTER if s < ROW_TILES else 0):
+                if squaring and c == EXP_AFTER:
                     take_exps(s - 1)
-                if s < ROW_TILES:
+                if squaring:
                     square(s, c)
                 if i >= 0:
-                    products.append(multiply(i, c, scale_banks))
-            if s < ROW_TILES:
+                    products.append(multiply(i, c, norm_banks if i == ROW_TILES - 1 else scale_banks))
+            if squaring:
                 find_radius(s)
             if i < 0:
                 continue
             find_factor(i)
+            by_bank = i == 0 or i >= ROW_TILES - 2
             for c in range(CHUNKS):
                 dest = result[:, i, 1 + c * BANK : 1 + (c + 1) * BANK]
-                if last and c % 2 == 1:
+                if on_scalar(i, c):
                     nc.scalar.activation(out=dest, in_=products[c][:], func=ACT.Copy, scale=factor[:, i : i + 1])
                 else:
                     nc.vector.tensor_scalar_mul(out=dest, in0=products[c][:], scalar1=factor[:, i : i + 1])
-                if last or c % 2 == 1:
-                    pieces = 1 if last else 2
+                if by_bank or c % 2 == 1:
+                    pieces = 1 if by_bank else 2
                     start = i * D + (c + 1 - pieces) * BANK
-                    end = ROW_TILES * (1 + D) if last and c + 1 == CHUNKS else i * D + (c + 1) * BANK
+                    end = ROW_TILES * (1 + D) if i == ROW_TILES - 1 and c + 1 == CHUNKS else i * D + (c + 1) * BANK
                     store(start, end)
+            if s == ROW_TILES:
+                take_exps(ROW_TILES - 1)

@@ -22,7 +22,7 @@ BANK = 512
 CHUNKS = D // BANK
 EPS = 1e-6
 VECTOR_COLS = 352
-EXP_AFTER = 3
+EXP_AFTER = 2
 
 FLOPS = 2 * ROWS * K * D
 
@@ -121,7 +121,9 @@ def tile_hgcn_pb_kernel(tc, x, w_sp, out):
         result = keep.tile([P, ROW_TILES, 1 + D], F32)
         result_flat = result[:].rearrange("p i c -> p (i c)")
         sumsq = keep.tile([P, ROW_TILES, CHUNKS], F32)
-        radius = keep.tile([P, ROW_TILES, 5], F32)
+        total = keep.tile([P, ROW_TILES], F32)
+        spare = keep.tile([P, CHUNKS], F32)
+        radius = keep.tile([P, ROW_TILES, 3], F32)
         expo = keep.tile([P, ROW_TILES, 2], F32)
         factor = keep.tile([P, ROW_TILES], F32)
 
@@ -146,40 +148,31 @@ def tile_hgcn_pb_kernel(tc, x, w_sp, out):
             )
 
         def find_radius(i):
-            nc.gpsimd.tensor_scalar(
-                out=radius[:, i, 0:1],
-                in0=sumsq[:, i, 0:1],
-                scalar1=sumsq[:, i, 1:2],
-                scalar2=sumsq[:, i, 2:3],
-                op0=ALU.add,
-                op1=ALU.add,
-            )
-            nc.gpsimd.tensor_scalar(
-                out=radius[:, i, 1:2],
-                in0=radius[:, i, 0:1],
-                scalar1=sumsq[:, i, 3:4],
-                scalar2=EPS * EPS,
-                op0=ALU.add,
-                op1=ALU.max,
+            nc.scalar.activation(
+                out=spare[:],
+                in_=sumsq[:, i, :],
+                func=ACT.Identity,
+                bias=EPS * EPS / CHUNKS,
+                accum_out=total[:, i : i + 1],
             )
             nc.gpsimd.tensor_tensor(
-                out=radius[:, i, 2:4], in0=radius[:, i, 1:2].to_broadcast([P, 2]), in1=powers[:], op=ALU.pow
+                out=radius[:, i, 0:2], in0=total[:, i : i + 1].to_broadcast([P, 2]), in1=powers[:], op=ALU.pow
             )
-            nc.gpsimd.tensor_scalar_mul(out=radius[:, i, 4:5], in0=radius[:, i, 3:4], scalar1=0.5)
+            nc.gpsimd.tensor_scalar_mul(out=radius[:, i, 2:3], in0=radius[:, i, 1:2], scalar1=0.5)
 
         def take_exps(i):
-            nc.scalar.activation(out=expo[:, i, 0:1], in_=radius[:, i, 2:3], func=ACT.Exp)
-            nc.scalar.activation(out=expo[:, i, 1:2], in_=radius[:, i, 2:3], func=ACT.Exp, scale=-1.0)
-
-        def find_factor(i):
-            nc.vector.scalar_tensor_tensor(
+            nc.scalar.activation(out=expo[:, i, 0:1], in_=radius[:, i, 0:1], func=ACT.Exp)
+            nc.scalar.activation(out=expo[:, i, 1:2], in_=radius[:, i, 0:1], func=ACT.Exp, scale=-1.0)
+            nc.gpsimd.tensor_scalar(
                 out=factor[:, i : i + 1],
                 in0=expo[:, i, 0:1],
-                scalar=expo[:, i, 1:2],
-                in1=radius[:, i, 4:5],
+                scalar1=expo[:, i, 1:2],
+                scalar2=radius[:, i, 2:3],
                 op0=ALU.subtract,
                 op1=ALU.mult,
             )
+
+        def find_factor(i):
             nc.vector.tensor_scalar(
                 out=result[:, i, 0:1],
                 in0=expo[:, i, 0:1],

@@ -163,16 +163,16 @@ def tile_hgcn_pb_kernel(tc, x, w_sp, out):
         def take_exps(i):
             nc.scalar.activation(out=expo[:, i, 0:1], in_=radius[:, i, 0:1], func=ACT.Exp)
             nc.scalar.activation(out=expo[:, i, 1:2], in_=radius[:, i, 0:1], func=ACT.Exp, scale=-1.0)
-            nc.gpsimd.tensor_scalar(
+
+        def find_factor(i):
+            nc.vector.scalar_tensor_tensor(
                 out=factor[:, i : i + 1],
                 in0=expo[:, i, 0:1],
-                scalar1=expo[:, i, 1:2],
-                scalar2=radius[:, i, 2:3],
+                scalar=expo[:, i, 1:2],
+                in1=radius[:, i, 2:3],
                 op0=ALU.subtract,
                 op1=ALU.mult,
             )
-
-        def find_factor(i):
             nc.vector.tensor_scalar(
                 out=result[:, i, 0:1],
                 in0=expo[:, i, 0:1],
@@ -233,7 +233,10 @@ def tile_hgcn_pb_kernel(tc, x, w_sp, out):
                 if by_bank or c % 2 == 1:
                     pieces = 1 if by_bank else 2
                     start = i * D + (c + 1 - pieces) * BANK
-                    end = ROW_TILES * (1 + D) if i == ROW_TILES - 1 and c + 1 == CHUNKS else i * D + (c + 1) * BANK
+                    end = i * D + (c + 1) * BANK
+                    if i == ROW_TILES - 1:
+                        start += ROW_TILES if c > 0 else 0
+                        end += ROW_TILES
                     store(start, end)
             if s == ROW_TILES:
                 take_exps(ROW_TILES - 1)

@@ -22,6 +22,8 @@ BANK = 512
 CHUNKS = D // BANK
 EPS = 1e-6
 VECTOR_COLS = 352
+WARM_START = 4
+WARM_CHUNK = 2
 EXP_AFTER = 2
 
 FLOPS = 2 * ROWS * K * D
@@ -63,6 +65,16 @@ def tile_hgcn_pb_kernel(tc, x, w_sp, out):
         nc.vector.memset(warm[:, 0:1], 0.0)
         nc.scalar.activation(out=warm[:, 1:2], in_=warm[:, 0:1], func=ACT.Exp)
 
+        zeros = keep.tile([P, BANK], BF16)
+        nc.vector.memset(zeros[:], 0.0)
+
+        def keep_warm(label, count, moving):
+            unread = scale_banks.tile([P, BANK], F32, name="unread_%s" % label, tag="bank")
+            for n in range(count):
+                nc.tensor.matmul(out=unread[:], lhsT=zeros[:, :P], rhs=moving, start=True, stop=True)
+
+        keep_warm("start", WARM_START, zeros[:])
+
         x_words = x_raw[:].bitcast(F32).rearrange("p i (q u) -> p i u q", u=2)
         x_grouped = keep.tile([P, ROW_TILES, P, PACK], BF16, align_bytes=64)
         x_grouped_words = x_grouped[:].bitcast(F32)
@@ -101,6 +113,7 @@ def tile_hgcn_pb_kernel(tc, x, w_sp, out):
                 [P, BANK, PACK], BF16, name="w_grouped%d" % c, tag="w_grouped", align_bytes=64
             )
             w_grouped.append(grouped)
+            keep_warm("w%d" % c, WARM_CHUNK, w_raw[c][:, 0, :])
             nc.vector.tensor_copy(
                 out=grouped[:, :VECTOR_COLS, :].rearrange("p (c i) t -> p c t i", i=4),
                 in_=w_raw[c][:, :, :VECTOR_COLS].rearrange("p t (c i) -> p c t i", i=4),

from contextlib import ExitStack

import concourse.mybir as mybir
from concourse.masks import make_identity

F32 = mybir.dt.float32
BF16 = mybir.dt.bfloat16
U32 = mybir.dt.uint32
U8 = mybir.dt.uint8
FP8X4 = mybir.dt.float8_e4m3fn_x4
ALU = mybir.AluOpType
ACT = mybir.ActivationFunctionType

P = 128
PACK = 4
K = P * PACK
ROWS = 1024
ROW_TILES = ROWS // P
PAIRS = ROW_TILES // 2
D = 2048
BANK = 512
CHUNKS = D // BANK
EPS = 1e-6
VECTOR_COLS = 352
WARM_START = 4
WARM_CHUNK = 2
EXP_AFTER = 2

FLOPS = 2 * ROWS * K * D


def tile_hgcn_pb_kernel(tc, x, w_sp, out):
    nc = tc.nc
    x_rows = x.flatten_outer_dims().rearrange("(p i) k -> p i k", i=ROW_TILES)
    out_flat = out.flatten_outer_dims().rearrange("(p i) c -> p (i c)", i=ROW_TILES)
    w_rows = w_sp.rearrange("(p t) c -> p t c", t=PACK)

    with ExitStack() as ctx:
        keep = ctx.enter_context(tc.tile_pool(name="keep", bufs=1))
        stage = ctx.enter_context(tc.tile_pool(name="stage", bufs=CHUNKS))
        norm_banks = ctx.enter_context(tc.psum_pool(name="norm_banks", bufs=4))
        scale_banks = ctx.enter_context(tc.psum_pool(name="scale_banks", bufs=4))
        ctx.enter_context(tc.manual_schedule())

        x_raw = keep.tile([P, ROW_TILES, K], BF16)
        w_raw = []

        def load_x(b):
            nc.sync.dma_start(out=x_raw[:, 2 * b : 2 * b + 2, :], in_=x_rows[:, 2 * b : 2 * b + 2, :])

        load_x(0)
        for c in range(CHUNKS):
            raw = stage.tile([P, PACK, BANK], BF16, name="w_raw%d" % c, tag="w_raw")
            nc.sync.dma_start(out=raw[:], in_=w_rows[:, :, c * BANK : (c + 1) * BANK])
            w_raw.append(raw)
        for b in range(1, PAIRS):
            load_x(b)

        ident = keep.tile([P, P], F32)
        make_identity(nc, ident[:])
        powers = keep.tile([P, 2], F32)
        nc.vector.memset(powers[:, 0:1], 0.5)
        nc.vector.memset(powers[:, 1:2], -0.5)
        warm = keep.tile([P, 2], F32)
        nc.vector.memset(warm[:, 0:1], 0.0)
        nc.scalar.activation(out=warm[:, 1:2], in_=warm[:, 0:1], func=ACT.Exp)

        zeros = keep.tile([P, BANK], BF16)
        nc.vector.memset(zeros[:], 0.0)

        def keep_warm(label, count, moving):
            unread = scale_banks.tile([P, BANK], F32, name="unread_%s" % label, tag="bank")
            for n in range(count):
                nc.tensor.matmul(out=unread[:], lhsT=zeros[:, :P], rhs=moving, start=True, stop=True)

        keep_warm("start", WARM_START, zeros[:])

        x_words = x_raw[:].bitcast(F32).rearrange("p i (q u) -> p i u q", u=2)
        x_grouped = keep.tile([P, ROW_TILES, P, PACK], BF16, align_bytes=64)
        x_grouped_words = x_grouped[:].bitcast(F32)
        x_codes = keep.tile([P, ROWS], U32, align_bytes=64)
        x_scales = keep.tile([P, ROWS], U8, align_bytes=64)

        x_transposed = {}

        def transpose_x(b, banks):
            xt = banks.tile([P, 2, 2, P], F32, name="xt%d" % b, tag="bank")
            x_transposed[b] = xt
            for i in range(2):
                for u in range(2):
                    nc.tensor.transpose(xt[:, i, u, :], x_words[:, 2 * b + i, u, :], ident[:])

        def group_x(b, copy):
            copy(
                out=x_grouped_words[:, 2 * b : 2 * b + 2, :, :],
                in_=x_transposed[b][:].rearrange("q i u r -> q i r u"),
            )

        def quantise_x(b):
            cols = slice(2 * b * P, (2 * b + 2) * P)
            nc.vector.quantize_mx(
                out=x_codes[:, cols].bitcast(FP8X4),
                scales=x_scales[:, cols],
                in_=x_grouped[:, 2 * b : 2 * b + 2, :, :].rearrange("p i r t -> p (i r t)"),
            )

        w_codes = keep.tile([P, D], U32, align_bytes=64)
        w_scales = keep.tile([P, D], U8, align_bytes=64)
        w_grouped = []

        def regroup(c):
            grouped = stage.tile(
                [P, BANK, PACK], BF16, name="w_grouped%d" % c, tag="w_grouped", align_bytes=64
            )
            w_grouped.append(grouped)
            keep_warm("w%d" % c, WARM_CHUNK, w_raw[c][:, 0, :])
            nc.vector.tensor_copy(
                out=grouped[:, :VECTOR_COLS, :].rearrange("p (c i) t -> p c t i", i=4),
                in_=w_raw[c][:, :, :VECTOR_COLS].rearrange("p t (c i) -> p c t i", i=4),
            )
            nc.scalar.copy(
                out=grouped[:, VECTOR_COLS:, :].rearrange("p (c i) t -> p c t i", i=4),
                in_=w_raw[c][:, :, VECTOR_COLS:].rearrange("p t (c i) -> p c t i", i=4),
            )

        def quantise_w(c):
            cols = slice(c * BANK, (c + 1) * BANK)
            nc.vector.quantize_mx(
                out=w_codes[:, cols].bitcast(FP8X4),
                scales=w_scales[:, cols],
                in_=w_grouped[c][:].rearrange("p c t -> p (c t)"),
            )

        result = keep.tile([P, ROW_TILES, 1 + D], F32)
        result_flat = result[:].rearrange("p i c -> p (i c)")
        sumsq = keep.tile([P, ROW_TILES, CHUNKS], F32)
        total = keep.tile([P, ROW_TILES], F32)
        spare = keep.tile([P, CHUNKS], F32)
        radius = keep.tile([P, ROW_TILES, 3], F32)
        expo = keep.tile([P, ROW_TILES, 2], F32)
        factor = keep.tile([P, ROW_TILES], F32)

        def multiply(i, c, banks):
            bank = banks.tile([P, BANK], F32, name="us%d_%d" % (i, c), tag="bank")
            nc.tensor.matmul_mx(
                out=bank[:],
                lhsT=x_codes[:, i * P : (i + 1) * P].bitcast(FP8X4),
                lhsT_scale=x_scales[:, i * P : (i + 1) * P],
                rhs=w_codes[:, c * BANK : (c + 1) * BANK].bitcast(FP8X4),
                rhs_scale=w_scales[:, c * BANK : (c + 1) * BANK],
                start=True,
                stop=True,
            )
            return bank

        def square(i, c):
            bank = multiply(i, c, norm_banks)
            squares = stage.tile([P, BANK], BF16, name="squares%d_%d" % (i, c), tag="squares")
            nc.scalar.activation(
                out=squares[:], in_=bank[:], func=ACT.Square, accum_out=sumsq[:, i, c : c + 1]
            )

        def find_radius(i):
            nc.scalar.activation(
                out=spare[:],
                in_=sumsq[:, i, :],
                func=ACT.Identity,
                bias=EPS * EPS / CHUNKS,
                accum_out=total[:, i : i + 1],
            )
            nc.gpsimd.tensor_tensor(
                out=radius[:, i, 0:2], in0=total[:, i : i + 1].to_broadcast([P, 2]), in1=powers[:], op=ALU.pow
            )
            nc.gpsimd.tensor_scalar_mul(out=radius[:, i, 2:3], in0=radius[:, i, 1:2], scalar1=0.5)

        def take_exps(i):
            nc.scalar.activation(out=expo[:, i, 0:1], in_=radius[:, i, 0:1], func=ACT.Exp)
            nc.scalar.activation(out=expo[:, i, 1:2], in_=radius[:, i, 0:1], func=ACT.Exp, scale=-1.0)

        def find_factor(i):
            nc.vector.scalar_tensor_tensor(
                out=factor[:, i : i + 1],
                in0=expo[:, i, 0:1],
                scalar=expo[:, i, 1:2],
                in1=radius[:, i, 2:3],
                op0=ALU.subtract,
                op1=ALU.mult,
            )
            nc.vector.tensor_scalar(
                out=result[:, i, 0:1],
                in0=expo[:, i, 0:1],
                scalar1=expo[:, i, 1:2],
                scalar2=0.5,
                op0=ALU.add,
                op1=ALU.mult,
            )

        def store(start, end):
            nc.sync.dma_start(out=out_flat[:, start:end], in_=result_flat[:, start:end])

        transpose_x(0, norm_banks)
        group_x(0, nc.scalar.copy)
        regroup(0)
        quantise_x(0)
        regroup(1)
        for c in range(CHUNKS):
            quantise_w(c)
            if c + 2 < CHUNKS:
                regroup(c + 2)
            square(0, c)
            if c > 0:
                transpose_x(c, scale_banks)
        find_radius(0)
        group_x(1, nc.vector.tensor_copy)
        for b in range(2, PAIRS):
            group_x(b, nc.vector.tensor_copy)
            quantise_x(b - 1)
        quantise_x(PAIRS - 1)

        def on_scalar(i, c):
            return (i == ROW_TILES - 1 and c % 2 == 1) or (i == ROW_TILES - 2 and c >= CHUNKS - 2)

        for s in range(1, ROW_TILES + 2):
            i = s - 2
            squaring = s < ROW_TILES
            products = []
            for c in range(CHUNKS):
                if squaring and c == EXP_AFTER:
                    take_exps(s - 1)
                if squaring:
                    square(s, c)
                if i >= 0:
                    products.append(multiply(i, c, norm_banks if i == ROW_TILES - 1 else scale_banks))
            if squaring:
                find_radius(s)
            if i < 0:
                continue
            find_factor(i)
            by_bank = i == 0 or i >= ROW_TILES - 2
            for c in range(CHUNKS):
                dest = result[:, i, 1 + c * BANK : 1 + (c + 1) * BANK]
                if on_scalar(i, c):
                    nc.scalar.activation(out=dest, in_=products[c][:], func=ACT.Copy, scale=factor[:, i : i + 1])
                else:
                    nc.vector.tensor_scalar_mul(out=dest, in0=products[c][:], scalar1=factor[:, i : i + 1])
                if by_bank or c % 2 == 1:
                    pieces = 1 if by_bank else 2
                    start = i * D + (c + 1 - pieces) * BANK
                    end = i * D + (c + 1) * BANK
                    if i == ROW_TILES - 1:
                        start += ROW_TILES if c > 0 else 0
                        end += ROW_TILES
                    store(start, end)
            if s == ROW_TILES:
                take_exps(ROW_TILES - 1)
